import numpy as np
import ml_dtypes


def mxq(x, axis, fmt="e4m3"):
    dtype, down = {"e4m3": (ml_dtypes.float8_e4m3fn, 7), "e5m2": (ml_dtypes.float8_e5m2, 14)}[fmt]
    v = np.moveaxis(np.asarray(x, np.float32).astype(ml_dtypes.bfloat16).astype(np.float64), axis, -1)
    blocks = v.reshape(v.shape[:-1] + (-1, 32))
    amax = np.abs(blocks).max(-1, keepdims=True)
    byte = np.maximum(np.where(amax > 0, np.frexp(amax)[1] - 1 + 127, 0) - down, 1)
    scale = np.exp2(byte - 127.0)
    codes = (blocks / scale).astype(np.float32).astype(dtype).astype(np.float64)
    return np.moveaxis((codes * scale).reshape(v.shape), -1, axis)


WIDE = False


def mx_kscale(k):
    if not WIDE:
        return np.ones(k)
    levels = np.array([10, -10, 5, -5, 0])
    if k % 512:
        return np.exp2(np.random.permutation(np.resize(levels, k // 32))).repeat(32)
    a = np.empty((k // 512, 16))
    for p in range(k // 512):
        a[p, :8] = np.random.permutation(np.resize(levels, 8))
        for g in range(8):
            far = levels[np.abs(levels - a[p, g]) >= 10]
            a[p, g + 8] = far[np.random.randint(len(far))]
    return np.exp2(a.ravel()).repeat(32)


BF16 = ml_dtypes.bfloat16


def bf(x):
    return np.asarray(x, np.float32).astype(BF16)


def f64(x):
    return np.asarray(x).astype(np.float64)


E2M1 = np.array([0.0, 0.5, 1.0, 1.5, 2.0, 3.0, 4.0, 6.0, -0.0, -0.5, -1.0, -1.5, -2.0, -3.0, -4.0, -6.0])


def pack_weight(w, fmt):
    k, n = w.shape
    w = f64(bf(w)).reshape(k // 32, 32, n)
    amax = np.abs(w).max(1)
    if fmt == "e4m3":
        byte = np.frexp(amax)[1] - 1 + 127 - 7
    else:
        mant, ex = np.frexp(amax / 6.0)
        byte = np.where(mant > 0.5, ex, ex - 1) + 127
    byte = np.clip(np.where(amax > 0, byte, 1), 1, 254)
    scaled = (w * np.exp2(127.0 - byte)[:, None, :]).reshape(k, n).astype(np.float32)
    by_word = np.ascontiguousarray(scaled.reshape(k // 512, 128, 4, n).transpose(0, 1, 3, 2))
    if fmt == "e4m3":
        words = by_word.astype(ml_dtypes.float8_e4m3fn).view(np.uint8)
    else:
        c = by_word.astype(ml_dtypes.float4_e2m1fn).view(np.uint8) & 0xF
        words = c[..., 0::2] | (c[..., 1::2] << 4)
    return np.ascontiguousarray(words), np.ascontiguousarray(byte.astype(np.uint8).reshape(k // 512, 16, n))


def unpack_weight(words, scales, fmt):
    g, p, n, _ = words.shape
    if fmt == "e4m3":
        vals = np.ascontiguousarray(words).view(ml_dtypes.float8_e4m3fn).astype(np.float64)
    else:
        nib = np.empty((g, p, n, 4), np.uint8)
        nib[..., 0::2] = words & 0xF
        nib[..., 1::2] = words >> 4
        vals = E2M1[nib]
    vals = vals * np.repeat(np.exp2(scales.astype(np.float64) - 127.0), 8, axis=1)[..., None]
    return vals.transpose(0, 1, 3, 2).reshape(g * 512, n)
def pack4(w):
    words, scales = pack_weight(w, "e2m1")
    return words.reshape(words.shape[0], 128, -1), scales


def unpack4(words, scales):
    return unpack_weight(words.reshape(words.shape[0], 128, -1, 2), scales, "e2m1")


N, M, D, F = 1024, 1024, 1024, 1024


def draw0():
    s, t = mx_kscale(N), mx_kscale(D)
    adj = bf((np.random.standard_normal((M, N)) / np.sqrt(D) + np.eye(M, N)) * s)
    x = bf(np.random.standard_normal((N, D)) / s[:, None] * t)
    words, scales = pack4(np.random.standard_normal((D, F)) * np.sqrt(2.0 / D) / t[:, None])
    return {"adj": adj,
            "x": x,
            "weight_words": words,
            "weight_scales": scales}


def core(adj, x, weight_words, weight_scales):
    ax = mxq(f64(adj), 1, "e4m3") @ mxq(f64(x), 0, "e4m3")
    return mxq(ax, 1, "e4m3") @ unpack4(weight_words, weight_scales)


def e4m3fn_bytes(y):
    return np.clip(np.asarray(y, np.float64), -448.0, 448.0).astype(np.float32).astype(ml_dtypes.float8_e4m3fn).view(np.uint8)


def e4m3fn_values(b):
    return np.asarray(b, np.uint8).view(ml_dtypes.float8_e4m3fn).astype(np.float64)


def setup_inputs():
    d = draw0()
    x0 = np.asarray(d['adj']).astype(np.float64)
    s = (np.max(np.abs(x0), axis=(0,), keepdims=True) / 448.0).astype(np.float32)
    out = {}
    for k, v in d.items():
        if k == 'adj':
            out['adj_bytes'] = e4m3fn_bytes(x0 / s.astype(np.float64))
            out['adj_scale'] = s
        else:
            out[k] = v
    return out


def reference(adj_bytes, adj_scale, x, weight_words, weight_scales):
    return core(e4m3fn_values(adj_bytes) * adj_scale.astype(np.float64), x, weight_words, weight_scales)

@@ -1,0 +1,246 @@
+from contextlib import ExitStack
+
+import concourse.mybir as mybir
+from concourse.masks import make_identity
+
+F32 = mybir.dt.float32
+BF16 = mybir.dt.bfloat16
+U32 = mybir.dt.uint32
+I32 = mybir.dt.int32
+U8 = mybir.dt.uint8
+FP8 = mybir.dt.float8_e4m3fn
+FP8X4 = mybir.dt.float8_e4m3fn_x4
+FP4X4 = mybir.dt.float4_e2m1fn_x4
+MULT = mybir.AluOpType.mult
+
+P = 128
+N = 1024
+NB = 8
+FLOPS = 2 * 2 * N * N * N
+
+V_SHARE = 36
+
+
+def tile_graphconvolution_pb_w4_kernel(tc, adj_bytes, adj_scale, x, weight_words, weight_scales, out):
+    nc = tc.nc
+    with ExitStack() as ctx:
+        keep = ctx.enter_context(tc.tile_pool(name="keep", bufs=1))
+        rot = ctx.enter_context(tc.tile_pool(name="rot", bufs=8))
+        ps_t = ctx.enter_context(tc.psum_pool(name="ps_t", bufs=2))
+        ps_a = ctx.enter_context(tc.psum_pool(name="ps_a", bufs=3))
+        ps_o = ctx.enter_context(tc.psum_pool(name="ps_o", bufs=3))
+        ctx.enter_context(tc.manual_schedule())
+
+        sc_col = keep.tile([P, 8], F32)
+        nc.sync.dma_start(out=sc_col[:], in_=adj_scale.rearrange("o (p c) -> p (o c)", c=8))
+
+        xraw = {}
+
+        def load_x(g, h):
+            t = keep.tile([P, 4, 512], BF16, name="xraw%d%d" % (g, h), align_bytes=64)
+            nc.sync.dma_start(out=t[:], in_=x[512 * g : 512 * g + 512, 512 * h : 512 * h + 512].rearrange("(p t) d -> p t d", t=4))
+            xraw[g, h] = t
+
+        adj8 = {}
+        rows = {}
+
+        def load_adj(first, n):
+            t = keep.tile([P, n, N], U8, name="adjb%d" % first, align_bytes=64)
+            r = slice(P * first, P * (first + n))
+            nc.sync.dma_start(out=t[:], in_=adj_bytes[r, :].rearrange("(p k) j -> p k j", k=n))
+            o = out[r, :].rearrange("(p k) f -> p k f", k=n)
+            for i in range(n):
+                adj8[first + i] = t[:, i, :]
+                rows[first + i] = o[:, i, :]
+
+        load_x(0, 0)
+        load_adj(0, 1)
+        load_x(1, 0)
+        load_x(0, 1)
+        load_adj(1, 1)
+        load_x(1, 1)
+        load_adj(2, 2)
+
+        wsc = keep.tile([P, 2, N], U8, align_bytes=64)
+        nc.vector.memset(wsc[:].rearrange("p g n -> p (g n)").bitcast(I32), 0)
+        for q in range(4):
+            nc.sync.dma_start(
+                out=wsc[32 * q : 32 * q + 4, :, :].bitcast(I32),
+                in_=weight_scales[:, 4 * q : 4 * q + 4, :].rearrange("g q n -> q g n").bitcast(I32),
+            )
+        w = keep.tile([P, 2, 2 * N], U8, align_bytes=64)
+        nc.sync.dma_start(out=w[:].bitcast(I32), in_=weight_words.rearrange("g p n -> p g n").bitcast(I32))
+        load_adj(4, 4)
+
+        ident = keep.tile([P, P], F32)
+        make_identity(nc, ident[:])
+        scbc = keep.tile([P, N], F32, align_bytes=64)
+        for half in range(2):
+            bank = ps_t.tile([P, 4, P], F32, tag="tp")
+            for c in range(4):
+                nc.tensor.transpose(bank[:, c, :], sc_col[:, 4 * half + c : 4 * half + c + 1].to_broadcast([P, P]), ident[:])
+            dst = scbc[:].rearrange("q (p h c) -> q h p c", h=2, c=4)[:, half, :, :]
+            src = bank[:].rearrange("q c p -> q p c")
+            if half == 0:
+                nc.vector.tensor_copy(out=dst, in_=src)
+            else:
+                nc.scalar.copy(dst, src)
+
+        xcodes = keep.tile([P, 2, 2, 512], U32, align_bytes=64)
+        xscales = keep.tile([P, 2, 2, 512], U8, align_bytes=64)
+        xg = {}
+
+        def x_inter(g, h):
+            t = keep.tile([P, 2048], BF16, name="xg%d%d" % (g, h), align_bytes=64)
+            src = xraw[g, h][:].rearrange("p t (m i a) -> p m a i t", i=2, a=4)
+            dst = t[:].rearrange("p (a m i t) -> p m a i t", a=4, i=2, t=4)
+            nc.scalar.copy(dst[:, V_SHARE:], src[:, V_SHARE:])
+            nc.vector.tensor_copy(out=dst[:, :V_SHARE], in_=src[:, :V_SHARE])
+            xg[g, h] = t
+
+        def x_quant(g, h):
+            nc.vector.quantize_mx(out=xcodes[:, h, g, :].bitcast(FP8X4), scales=xscales[:, h, g, :], in_=xg[g, h][:])
+
+        prods, banks, grouped, acodes, ascales = {}, {}, {}, {}, {}
+
+        def prod(b):
+            pr = rot.tile([P, N], BF16, align_bytes=64)
+            nc.vector.tensor_tensor(out=pr[:], in0=adj8[b].bitcast(FP8), in1=scbc[:], op=MULT)
+            prods[b] = pr
+
+        def tp(b):
+            bank = ps_t.tile([P, 4, P], F32, tag="tp")
+            words = prods[b][:].bitcast(F32)
+            for g in range(2):
+                for u in range(2):
+                    nc.tensor.transpose(bank[:, 2 * g + u, :], words[:, 256 * g + u : 256 * g + 256 : 2], ident[:])
+            banks[b] = bank
+
+        def tcopy(b):
+            gr = rot.tile([P, N], BF16, align_bytes=64)
+            nc.scalar.copy(
+                gr[:].bitcast(F32).rearrange("p (g r u) -> p g r u", g=2, u=2),
+                banks[b][:].rearrange("p (g u) r -> p g r u", u=2),
+            )
+            grouped[b] = gr
+
+        def aq(b):
+            ac = rot.tile([P, 256], U32, align_bytes=64)
+            asc = rot.tile([P, 256], U8, align_bytes=64)
+            nc.vector.quantize_mx(out=ac[:].bitcast(FP8X4), scales=asc[:], in_=grouped[b][:])
+            acodes[b] = ac
+            ascales[b] = asc
+
+        ax_ps, axg, axc, axs = {}, {}, {}, {}
+
+        def s1(b, h):
+            acc = ps_a.tile([P, 4, P], F32)
+            for a in range(4):
+                cols = slice(P * a, P * a + P)
+                for g in range(2):
+                    nc.tensor.matmul_mx(
+                        out=acc[:, a, :],
+                        lhsT=xcodes[:, h, g, cols].bitcast(FP8X4),
+                        lhsT_scale=xscales[:, h, g, cols],
+                        rhs=acodes[b][:, P * g : P * g + P].bitcast(FP8X4),
+                        rhs_scale=ascales[b][:, P * g : P * g + P],
+                        start=(g == 0),
+                        stop=(g == 1),
+                    )
+            ax_ps[b, h] = acc
+
+        def ax_copy(b, h):
+            axt = rot.tile([P, 512], BF16, name="axt%d" % h, align_bytes=64)
+            src = ax_ps[b, h][:].rearrange("p a r -> p r a")
+            dst = axt[:].rearrange("p (r a) -> p r a", a=4)
+            if h == 0:
+                nc.scalar.copy(dst, src)
+            else:
+                nc.vector.tensor_copy(out=dst, in_=src)
+            axg[b, h] = axt
+
+        def axq(b, h):
+            if h == 0:
+                cod = rot.tile([P, 256], U32, align_bytes=64)
+                sca = rot.tile([P, 256], U8, align_bytes=64)
+                axc[b] = cod
+                axs[b] = sca
+            cols = slice(P * h, P * h + P)
+            nc.vector.quantize_mx(out=axc[b][:, cols].bitcast(FP8X4), scales=axs[b][:, cols], in_=axg[b, h][:])
+
+        o_ps, o_sb = {}, {}
+
+        def s2(b, f):
+            acc = ps_o.tile([P, 512], F32)
+            for h in range(2):
+                cols = slice(P * h, P * h + P)
+                nc.tensor.matmul_mx(
+                    out=acc[:],
+                    lhsT=axc[b][:, cols].bitcast(FP8X4),
+                    lhsT_scale=axs[b][:, cols],
+                    rhs=w[:, h, 1024 * f : 1024 * f + 1024].bitcast(FP4X4),
+                    rhs_scale=wsc[:, h, 512 * f : 512 * f + 512],
+                    start=(h == 0),
+                    stop=(h == 1),
+                )
+            o_ps[b, f] = acc
+
+        def o_copy(b, f):
+            if f == 0:
+                ot = rot.tile([P, N], F32)
+                o_sb[b] = ot
+            dst = o_sb[b][:, 512 * f : 512 * f + 512]
+            if f == 1 and b == NB - 1:
+                nc.vector.tensor_copy(out=dst, in_=o_ps[b, f][:])
+            else:
+                nc.scalar.copy(dst, o_ps[b, f][:])
+            if b == NB - 1:
+                nc.sync.dma_start(out=rows[b][:, 512 * f : 512 * f + 512], in_=dst)
+            elif f == 1:
+                nc.sync.dma_start(out=rows[b], in_=o_sb[b][:])
+
+        x_inter(0, 0)
+        prod(0)
+        x_quant(0, 0)
+        tp(0)
+        x_inter(1, 0)
+        tcopy(0)
+        aq(0)
+        x_quant(1, 0)
+        x_inter(0, 1)
+        s1(0, 0)
+        prod(1)
+        x_quant(0, 1)
+        tp(1)
+        x_inter(1, 1)
+        tcopy(1)
+        ax_copy(0, 0)
+        aq(1)
+        x_quant(1, 1)
+        s1(0, 1)
+        axq(0, 0)
+        prod(2)
+        ax_copy(0, 1)
+        axq(0, 1)
+
+        for b in range(NB):
+            if b + 2 < NB:
+                tp(b + 2)
+            if b + 1 < NB:
+                s1(b + 1, 0)
+                s1(b + 1, 1)
+            if b + 3 < NB:
+                prod(b + 3)
+            if b + 2 < NB:
+                tcopy(b + 2)
+                aq(b + 2)
+            if b + 1 < NB:
+                ax_copy(b + 1, 0)
+                ax_copy(b + 1, 1)
+            s2(b, 0)
+            s2(b, 1)
+            if b + 1 < NB:
+                axq(b + 1, 0)
+                axq(b + 1, 1)
+            o_copy(b, 0)
+            o_copy(b, 1)

@@ -18,8 +18,6 @@ N = 1024
 NB = 8
 FLOPS = 2 * 2 * N * N * N
 
-V_SHARE = 36
-
 
 def tile_graphconvolution_pb_w4_kernel(tc, adj_bytes, adj_scale, x, weight_words, weight_scales, out):
     nc = tc.nc
@@ -31,8 +29,8 @@ def tile_graphconvolution_pb_w4_kernel(tc, adj_bytes, adj_scale, x, weight_words
         ps_o = ctx.enter_context(tc.psum_pool(name="ps_o", bufs=3))
         ctx.enter_context(tc.manual_schedule())
 
-        sc_col = keep.tile([P, 8], F32)
-        nc.sync.dma_start(out=sc_col[:], in_=adj_scale.rearrange("o (p c) -> p (o c)", c=8))
+        sc_col = keep.tile([P, 2, 4], F32)
+        nc.sync.dma_start(out=sc_col[:], in_=adj_scale.rearrange("o (h p c) -> p (o h) c", h=2, c=4))
 
         xraw = {}
 
@@ -75,28 +73,38 @@ def tile_graphconvolution_pb_w4_kernel(tc, adj_bytes, adj_scale, x, weight_words
         ident = keep.tile([P, P], F32)
         make_identity(nc, ident[:])
         scbc = keep.tile([P, N], F32, align_bytes=64)
-        for half in range(2):
-            bank = ps_t.tile([P, 4, P], F32, tag="tp")
-            for c in range(4):
-                nc.tensor.transpose(bank[:, c, :], sc_col[:, 4 * half + c : 4 * half + c + 1].to_broadcast([P, P]), ident[:])
-            dst = scbc[:].rearrange("q (p h c) -> q h p c", h=2, c=4)[:, half, :, :]
-            src = bank[:].rearrange("q c p -> q p c")
+        sc_banks = []
+
+        def sc_transposes():
+            for half in range(2):
+                bank = ps_t.tile([P, 4, P], F32, tag="tp")
+                for c in range(4):
+                    nc.tensor.transpose(bank[:, c, :], sc_col[:, half, c : c + 1].to_broadcast([P, P]), ident[:])
+                sc_banks.append(bank)
+
+        def sc_copy(half):
+            dst = scbc[:, 512 * half : 512 * half + 512].rearrange("q (p c) -> q p c", c=4)
+            src = sc_banks[half][:].rearrange("q c p -> q p c")
             if half == 0:
                 nc.vector.tensor_copy(out=dst, in_=src)
             else:
                 nc.scalar.copy(dst, src)
 
+
         xcodes = keep.tile([P, 2, 2, 512], U32, align_bytes=64)
         xscales = keep.tile([P, 2, 2, 512], U8, align_bytes=64)
         xg = {}
 
-        def x_inter(g, h):
-            t = keep.tile([P, 2048], BF16, name="xg%d%d" % (g, h), align_bytes=64)
-            src = xraw[g, h][:].rearrange("p t (m i a) -> p m a i t", i=2, a=4)
-            dst = t[:].rearrange("p (a m i t) -> p m a i t", a=4, i=2, t=4)
-            nc.scalar.copy(dst[:, V_SHARE:], src[:, V_SHARE:])
-            nc.vector.tensor_copy(out=dst[:, :V_SHARE], in_=src[:, :V_SHARE])
-            xg[g, h] = t
+        def x_inter(eng, g, h, lo, hi):
+            if (g, h) not in xg:
+                t = keep.tile([P, 2048], BF16, name="xg%d%d" % (g, h), align_bytes=64)
+                xg[g, h] = t
+            src = xraw[g, h][:].rearrange("p t (m i a) -> p m a i t", i=2, a=4)[:, lo:hi]
+            dst = xg[g, h][:].rearrange("p (a m i t) -> p m a i t", a=4, i=2, t=4)[:, lo:hi]
+            if eng == "V":
+                nc.vector.tensor_copy(out=dst, in_=src)
+            else:
+                nc.scalar.copy(dst, src)
 
         def x_quant(g, h):
             nc.vector.quantize_mx(out=xcodes[:, h, g, :].bitcast(FP8X4), scales=xscales[:, h, g, :], in_=xg[g, h][:])
@@ -153,14 +161,11 @@ def tile_graphconvolution_pb_w4_kernel(tc, adj_bytes, adj_scale, x, weight_words
             axt = rot.tile([P, 512], BF16, name="axt%d" % h, align_bytes=64)
             src = ax_ps[b, h][:].rearrange("p a r -> p r a")
             dst = axt[:].rearrange("p (r a) -> p r a", a=4)
-            if h == 0:
-                nc.scalar.copy(dst, src)
-            else:
-                nc.vector.tensor_copy(out=dst, in_=src)
+            nc.scalar.copy(dst, src)
             axg[b, h] = axt
 
         def axq(b, h):
-            if h == 0:
+            if b not in axc:
                 cod = rot.tile([P, 256], U32, align_bytes=64)
                 sca = rot.tile([P, 256], U8, align_bytes=64)
                 axc[b] = cod
@@ -189,8 +194,18 @@ def tile_graphconvolution_pb_w4_kernel(tc, adj_bytes, adj_scale, x, weight_words
             if f == 0:
                 ot = rot.tile([P, N], F32)
                 o_sb[b] = ot
+            if b == NB - 1 and f == 1:
+                for z in range(2):
+                    cols = slice(512 + 256 * z, 768 + 256 * z)
+                    part = o_ps[b, f][:, 256 * z : 256 * z + 256]
+                    if z == 0:
+                        nc.vector.tensor_copy(out=o_sb[b][:, cols], in_=part)
+                    else:
+                        nc.scalar.copy(o_sb[b][:, cols], part)
+                    nc.sync.dma_start(out=rows[b][:, cols], in_=o_sb[b][:, cols])
+                return
             dst = o_sb[b][:, 512 * f : 512 * f + 512]
-            if f == 1 and b == NB - 1:
+            if b % 2 == 0 or f == 1:
                 nc.vector.tensor_copy(out=dst, in_=o_ps[b, f][:])
             else:
                 nc.scalar.copy(dst, o_ps[b, f][:])
@@ -199,48 +214,80 @@ def tile_graphconvolution_pb_w4_kernel(tc, adj_bytes, adj_scale, x, weight_words
             elif f == 1:
                 nc.sync.dma_start(out=rows[b], in_=o_sb[b][:])
 
-        x_inter(0, 0)
+        def s_xi(g, h, lo, hi):
+            x_inter("S", g, h, lo, hi)
+
+        def v_xi(g, h, lo, hi):
+            x_inter("V", g, h, lo, hi)
+
+        v_xi(0, 0, 0, 32)
+        sc_transposes()
+        s_xi(0, 0, 48, 64)
+        sc_copy(1)
+        sc_copy(0)
+        s_xi(1, 0, 0, 64)
+        v_xi(0, 0, 32, 48)
         prod(0)
         x_quant(0, 0)
+        v_xi(0, 1, 48, 64)
         tp(0)
-        x_inter(1, 0)
+        s_xi(0, 1, 0, 16)
         tcopy(0)
-        aq(0)
-        x_quant(1, 0)
-        x_inter(0, 1)
-        s1(0, 0)
         prod(1)
-        x_quant(0, 1)
+        s_xi(1, 1, 0, 16)
         tp(1)
-        x_inter(1, 1)
         tcopy(1)
-        ax_copy(0, 0)
-        aq(1)
-        x_quant(1, 1)
-        s1(0, 1)
-        axq(0, 0)
+        s_xi(0, 1, 16, 32)
+        x_quant(1, 0)
         prod(2)
+        s_xi(1, 1, 16, 32)
+        prod(3)
+        tp(2)
+        aq(0)
+        tp(3)
+        v_xi(1, 1, 48, 64)
+        aq(1)
+        s_xi(0, 1, 32, 48)
+        s_xi(1, 1, 32, 48)
+        x_quant(0, 1)
+        tcopy(2)
+        x_quant(1, 1)
+        s1(0, 0)
+        ax_copy(0, 0)
+        s1(1, 0)
+        aq(2)
+        ax_copy(1, 0)
+        prod(4)
+        s1(0, 1)
         ax_copy(0, 1)
+        prod(5)
+        s1(1, 1)
+        s1(2, 1)
+        s1(2, 0)
+        tp(4)
+        tcopy(3)
+        axq(0, 0)
         axq(0, 1)
+        ax_copy(1, 1)
+
+        def at(fn, b, *args):
+            if 0 <= b < NB:
+                fn(b, *args)
 
         for b in range(NB):
-            if b + 2 < NB:
-                tp(b + 2)
-            if b + 1 < NB:
-                s1(b + 1, 0)
-                s1(b + 1, 1)
-            if b + 3 < NB:
-                prod(b + 3)
-            if b + 2 < NB:
-                tcopy(b + 2)
-                aq(b + 2)
-            if b + 1 < NB:
-                ax_copy(b + 1, 0)
-                ax_copy(b + 1, 1)
+            at(tp, b + 5)
+            at(axq, b + 1, 1)
+            at(tcopy, b + 4)
+            at(aq, b + 3)
+            at(s1, b + 3, 1)
+            at(axq, b + 1, 0)
+            at(ax_copy, b + 2, 1)
             s2(b, 0)
+            at(o_copy, b - 1, 0)
             s2(b, 1)
-            if b + 1 < NB:
-                axq(b + 1, 0)
-                axq(b + 1, 1)
-            o_copy(b, 0)
-            o_copy(b, 1)
+            at(prod, b + 6)
+            at(s1, b + 3, 0)
+            at(o_copy, b - 1, 1)
+            at(ax_copy, b + 2, 0)
+        o_copy(NB - 1, 0)
+        o_copy(NB - 1, 1)

@@ -176,7 +176,7 @@ def tile_graphconvolution_pb_w4_kernel(tc, adj_bytes, adj_scale, x, weight_words
         o_ps, o_sb = {}, {}
 
         def s2(b, f):
-            acc = ps_o.tile([P, 512], F32)
+            acc = ps_o.tile([P, 512], F32, tag="acc")
             for h in range(2):
                 cols = slice(P * h, P * h + P)
                 nc.tensor.matmul_mx(
@@ -209,10 +209,15 @@ def tile_graphconvolution_pb_w4_kernel(tc, adj_bytes, adj_scale, x, weight_words
                 nc.vector.tensor_copy(out=dst, in_=o_ps[b, f][:])
             else:
                 nc.scalar.copy(dst, o_ps[b, f][:])
-            if b == NB - 1:
-                nc.sync.dma_start(out=rows[b][:, 512 * f : 512 * f + 512], in_=dst)
-            elif f == 1:
-                nc.sync.dma_start(out=rows[b], in_=o_sb[b][:])
+            nc.sync.dma_start(out=rows[b][:, 512 * f : 512 * f + 512], in_=dst)
+
+        ones = keep.tile([P, 512], BF16, align_bytes=64)
+        nc.vector.memset(ones[:], 1.0)
+
+        def warm(n):
+            for i in range(n):
+                acc = ps_o.tile([P, 512], F32, tag="acc")
+                nc.tensor.matmul(acc[:], lhsT=ones[:, 0:P], rhs=ones[:], start=True, stop=True)
 
         def s_xi(g, h, lo, hi):
             x_inter("S", g, h, lo, hi)
@@ -231,11 +236,13 @@ def tile_graphconvolution_pb_w4_kernel(tc, adj_bytes, adj_scale, x, weight_words
         x_quant(0, 0)
         v_xi(0, 1, 48, 64)
         tp(0)
+        warm(2)
         s_xi(0, 1, 0, 16)
         tcopy(0)
         prod(1)
         s_xi(1, 1, 0, 16)
         tp(1)
+        warm(2)
         tcopy(1)
         s_xi(0, 1, 16, 32)
         x_quant(1, 0)
@@ -243,8 +250,10 @@ def tile_graphconvolution_pb_w4_kernel(tc, adj_bytes, adj_scale, x, weight_words
         s_xi(1, 1, 16, 32)
         prod(3)
         tp(2)
+        warm(1)
         aq(0)
         tp(3)
+        warm(1)
         v_xi(1, 1, 48, 64)
         aq(1)
         s_xi(0, 1, 32, 48)

@@ -16,6 +16,7 @@ MULT = mybir.AluOpType.mult
 P = 128
 N = 1024
 NB = 8
+PERM_FROM = 4
 FLOPS = 2 * 2 * N * N * N
 
 
@@ -116,12 +117,27 @@ def tile_graphconvolution_pb_w4_kernel(tc, adj_bytes, adj_scale, x, weight_words
             nc.vector.tensor_tensor(out=pr[:], in0=adj8[b].bitcast(FP8), in1=scbc[:], op=MULT)
             prods[b] = pr
 
+        def perm(b):
+            if b >= PERM_FROM:
+                pr = prods[b]
+                pm = rot.tile([P, N], BF16, align_bytes=64)
+                nc.vector.tensor_copy(
+                    out=pm[:].bitcast(F32).rearrange("p (g u w) -> p g u w", g=2, u=2),
+                    in_=pr[:].bitcast(F32).rearrange("p (g w u) -> p g u w", g=2, u=2),
+                )
+                prods[b] = pm
+
         def tp(b):
             bank = ps_t.tile([P, 4, P], F32, tag="tp")
             words = prods[b][:].bitcast(F32)
             for g in range(2):
                 for u in range(2):
-                    nc.tensor.transpose(bank[:, 2 * g + u, :], words[:, 256 * g + u : 256 * g + 256 : 2], ident[:])
+                    lo = 256 * g
+                    if b >= PERM_FROM:
+                        cols = slice(lo + 128 * u, lo + 128 * u + 128)
+                    else:
+                        cols = slice(lo + u, lo + 256, 2)
+                    nc.tensor.transpose(bank[:, 2 * g + u, :], words[:, cols], ident[:])
             banks[b] = bank
 
         def tcopy(b):
@@ -161,7 +177,10 @@ def tile_graphconvolution_pb_w4_kernel(tc, adj_bytes, adj_scale, x, weight_words
             axt = rot.tile([P, 512], BF16, name="axt%d" % h, align_bytes=64)
             src = ax_ps[b, h][:].rearrange("p a r -> p r a")
             dst = axt[:].rearrange("p (r a) -> p r a", a=4)
-            nc.scalar.copy(dst, src)
+            if b >= 2 and b % 2 == 1 and h == 0:
+                nc.vector.tensor_copy(out=dst, in_=src)
+            else:
+                nc.scalar.copy(dst, src)
             axg[b, h] = axt
 
         def axq(b, h):
@@ -205,7 +224,7 @@ def tile_graphconvolution_pb_w4_kernel(tc, adj_bytes, adj_scale, x, weight_words
                     nc.sync.dma_start(out=rows[b][:, cols], in_=o_sb[b][:, cols])
                 return
             dst = o_sb[b][:, 512 * f : 512 * f + 512]
-            if b % 2 == 0 or f == 1:
+            if f == 1:
                 nc.vector.tensor_copy(out=dst, in_=o_ps[b, f][:])
             else:
                 nc.scalar.copy(dst, o_ps[b, f][:])
@@ -225,78 +244,81 @@ def tile_graphconvolution_pb_w4_kernel(tc, adj_bytes, adj_scale, x, weight_words
         def v_xi(g, h, lo, hi):
             x_inter("V", g, h, lo, hi)
 
-        v_xi(0, 0, 0, 32)
+        s_xi(0, 0, 0, 16)
         sc_transposes()
-        s_xi(0, 0, 48, 64)
-        sc_copy(1)
+        v_xi(0, 0, 32, 64)
+        s_xi(0, 0, 16, 32)
         sc_copy(0)
-        s_xi(1, 0, 0, 64)
-        v_xi(0, 0, 32, 48)
-        prod(0)
+        sc_copy(1)
         x_quant(0, 0)
-        v_xi(0, 1, 48, 64)
+        prod(0)
         tp(0)
         warm(2)
+        s_xi(1, 0, 16, 48)
+        s_xi(0, 1, 32, 48)
+        v_xi(0, 1, 48, 64)
+        s_xi(1, 0, 0, 16)
         s_xi(0, 1, 0, 16)
-        tcopy(0)
+        s_xi(1, 1, 16, 32)
+        v_xi(1, 0, 48, 64)
         prod(1)
-        s_xi(1, 1, 0, 16)
         tp(1)
         warm(2)
-        tcopy(1)
-        s_xi(0, 1, 16, 32)
-        x_quant(1, 0)
         prod(2)
-        s_xi(1, 1, 16, 32)
+        tcopy(0)
         prod(3)
+        tcopy(1)
+        aq(0)
+        s_xi(1, 1, 48, 64)
+        x_quant(1, 0)
         tp(2)
         warm(1)
-        aq(0)
+        v_xi(0, 1, 16, 32)
+        s_xi(1, 1, 0, 16)
+        aq(1)
         tp(3)
         warm(1)
-        v_xi(1, 1, 48, 64)
-        aq(1)
-        s_xi(0, 1, 32, 48)
-        s_xi(1, 1, 32, 48)
+        s1(0, 0)
+        s1(1, 0)
         x_quant(0, 1)
         tcopy(2)
-        x_quant(1, 1)
-        s1(0, 0)
-        ax_copy(0, 0)
-        s1(1, 0)
+        s_xi(1, 1, 32, 48)
         aq(2)
-        ax_copy(1, 0)
-        prod(4)
-        s1(0, 1)
-        ax_copy(0, 1)
-        prod(5)
-        s1(1, 1)
-        s1(2, 1)
         s1(2, 0)
-        tp(4)
-        tcopy(3)
+        x_quant(1, 1)
+        ax_copy(0, 0)
+        s1(0, 1)
+        ax_copy(1, 0)
+        s1(1, 1)
+        prod(4)
         axq(0, 0)
-        axq(0, 1)
+        perm(4)
+        tp(4)
+        ax_copy(0, 1)
+        s1(2, 1)
         ax_copy(1, 1)
+        tcopy(3)
+        axq(0, 1)
 
         def at(fn, b, *args):
             if 0 <= b < NB:
                 fn(b, *args)
 
         for b in range(NB):
-            at(tp, b + 5)
+            at(o_copy, b - 1, 0)
+            s2(b, 0)
+            at(axq, b + 1, 0)
             at(axq, b + 1, 1)
-            at(tcopy, b + 4)
+            s2(b, 1)
+            at(ax_copy, b + 2, 1)
             at(aq, b + 3)
             at(s1, b + 3, 1)
-            at(axq, b + 1, 0)
-            at(ax_copy, b + 2, 1)
-            s2(b, 0)
-            at(o_copy, b - 1, 0)
-            s2(b, 1)
-            at(prod, b + 6)
             at(s1, b + 3, 0)
+            at(tcopy, b + 4)
+            at(prod, b + 5)
             at(o_copy, b - 1, 1)
+            at(perm, b + 5)
+            at(tp, b + 5)
             at(ax_copy, b + 2, 0)
         o_copy(NB - 1, 0)
         o_copy(NB - 1, 1)

from contextlib import ExitStack

import concourse.mybir as mybir
from concourse.masks import make_identity

F32 = mybir.dt.float32
BF16 = mybir.dt.bfloat16
U32 = mybir.dt.uint32
I32 = mybir.dt.int32
U8 = mybir.dt.uint8
FP8 = mybir.dt.float8_e4m3fn
FP8X4 = mybir.dt.float8_e4m3fn_x4
FP4X4 = mybir.dt.float4_e2m1fn_x4
MULT = mybir.AluOpType.mult

P = 128
N = 1024
NB = 8
PERM_FROM = 4
FLOPS = 2 * 2 * N * N * N


def tile_graphconvolution_pb_w4_kernel(tc, adj_bytes, adj_scale, x, weight_words, weight_scales, out):
    nc = tc.nc
    with ExitStack() as ctx:
        keep = ctx.enter_context(tc.tile_pool(name="keep", bufs=1))
        rot = ctx.enter_context(tc.tile_pool(name="rot", bufs=8))
        ps_t = ctx.enter_context(tc.psum_pool(name="ps_t", bufs=2))
        ps_a = ctx.enter_context(tc.psum_pool(name="ps_a", bufs=3))
        ps_o = ctx.enter_context(tc.psum_pool(name="ps_o", bufs=3))
        ctx.enter_context(tc.manual_schedule())

        sc_col = keep.tile([P, 2, 4], F32)
        nc.sync.dma_start(out=sc_col[:], in_=adj_scale.rearrange("o (h p c) -> p (o h) c", h=2, c=4))

        xraw = {}

        def load_x(g, h):
            t = keep.tile([P, 4, 512], BF16, name="xraw%d%d" % (g, h), align_bytes=64)
            nc.sync.dma_start(out=t[:], in_=x[512 * g : 512 * g + 512, 512 * h : 512 * h + 512].rearrange("(p t) d -> p t d", t=4))
            xraw[g, h] = t

        adj8 = {}
        rows = {}

        def load_adj(first, n):
            t = keep.tile([P, n, N], U8, name="adjb%d" % first, align_bytes=64)
            r = slice(P * first, P * (first + n))
            nc.sync.dma_start(out=t[:], in_=adj_bytes[r, :].rearrange("(p k) j -> p k j", k=n))
            o = out[r, :].rearrange("(p k) f -> p k f", k=n)
            for i in range(n):
                adj8[first + i] = t[:, i, :]
                rows[first + i] = o[:, i, :]

        load_x(0, 0)
        load_adj(0, 1)
        load_x(1, 0)
        load_x(0, 1)
        load_adj(1, 1)
        load_x(1, 1)
        load_adj(2, 2)

        wsc = keep.tile([P, 2, N], U8, align_bytes=64)
        nc.vector.memset(wsc[:].rearrange("p g n -> p (g n)").bitcast(I32), 0)
        for q in range(4):
            nc.sync.dma_start(
                out=wsc[32 * q : 32 * q + 4, :, :].bitcast(I32),
                in_=weight_scales[:, 4 * q : 4 * q + 4, :].rearrange("g q n -> q g n").bitcast(I32),
            )
        w = keep.tile([P, 2, 2 * N], U8, align_bytes=64)
        nc.sync.dma_start(out=w[:].bitcast(I32), in_=weight_words.rearrange("g p n -> p g n").bitcast(I32))
        load_adj(4, 4)

        ident = keep.tile([P, P], F32)
        make_identity(nc, ident[:])
        scbc = keep.tile([P, N], F32, align_bytes=64)
        sc_banks = []

        def sc_transposes():
            for half in range(2):
                bank = ps_t.tile([P, 4, P], F32, tag="tp")
                for c in range(4):
                    nc.tensor.transpose(bank[:, c, :], sc_col[:, half, c : c + 1].to_broadcast([P, P]), ident[:])
                sc_banks.append(bank)

        def sc_copy(half):
            dst = scbc[:, 512 * half : 512 * half + 512].rearrange("q (p c) -> q p c", c=4)
            src = sc_banks[half][:].rearrange("q c p -> q p c")
            if half == 0:
                nc.vector.tensor_copy(out=dst, in_=src)
            else:
                nc.scalar.copy(dst, src)


        xcodes = keep.tile([P, 2, 2, 512], U32, align_bytes=64)
        xscales = keep.tile([P, 2, 2, 512], U8, align_bytes=64)
        xg = {}

        def x_inter(eng, g, h, lo, hi):
            if (g, h) not in xg:
                t = keep.tile([P, 2048], BF16, name="xg%d%d" % (g, h), align_bytes=64)
                xg[g, h] = t
            src = xraw[g, h][:].rearrange("p t (m i a) -> p m a i t", i=2, a=4)[:, lo:hi]
            dst = xg[g, h][:].rearrange("p (a m i t) -> p m a i t", a=4, i=2, t=4)[:, lo:hi]
            if eng == "V":
                nc.vector.tensor_copy(out=dst, in_=src)
            else:
                nc.scalar.copy(dst, src)

        def x_quant(g, h):
            nc.vector.quantize_mx(out=xcodes[:, h, g, :].bitcast(FP8X4), scales=xscales[:, h, g, :], in_=xg[g, h][:])

        prods, banks, grouped, acodes, ascales = {}, {}, {}, {}, {}

        def prod(b):
            pr = rot.tile([P, N], BF16, align_bytes=64)
            nc.vector.tensor_tensor(out=pr[:], in0=adj8[b].bitcast(FP8), in1=scbc[:], op=MULT)
            prods[b] = pr

        def perm(b):
            if b >= PERM_FROM:
                pr = prods[b]
                pm = rot.tile([P, N], BF16, align_bytes=64)
                nc.vector.tensor_copy(
                    out=pm[:].bitcast(F32).rearrange("p (g u w) -> p g u w", g=2, u=2),
                    in_=pr[:].bitcast(F32).rearrange("p (g w u) -> p g u w", g=2, u=2),
                )
                prods[b] = pm

        def tp(b):
            bank = ps_t.tile([P, 4, P], F32, tag="tp")
            words = prods[b][:].bitcast(F32)
            for g in range(2):
                for u in range(2):
                    lo = 256 * g
                    if b >= PERM_FROM:
                        cols = slice(lo + 128 * u, lo + 128 * u + 128)
                    else:
                        cols = slice(lo + u, lo + 256, 2)
                    nc.tensor.transpose(bank[:, 2 * g + u, :], words[:, cols], ident[:])
            banks[b] = bank

        def tcopy(b):
            gr = rot.tile([P, N], BF16, align_bytes=64)
            nc.scalar.copy(
                gr[:].bitcast(F32).rearrange("p (g r u) -> p g r u", g=2, u=2),
                banks[b][:].rearrange("p (g u) r -> p g r u", u=2),
            )
            grouped[b] = gr

        def aq(b):
            ac = rot.tile([P, 256], U32, align_bytes=64)
            asc = rot.tile([P, 256], U8, align_bytes=64)
            nc.vector.quantize_mx(out=ac[:].bitcast(FP8X4), scales=asc[:], in_=grouped[b][:])
            acodes[b] = ac
            ascales[b] = asc

        ax_ps, axg, axc, axs = {}, {}, {}, {}

        def s1(b, h):
            acc = ps_a.tile([P, 4, P], F32)
            for a in range(4):
                cols = slice(P * a, P * a + P)
                for g in range(2):
                    nc.tensor.matmul_mx(
                        out=acc[:, a, :],
                        lhsT=xcodes[:, h, g, cols].bitcast(FP8X4),
                        lhsT_scale=xscales[:, h, g, cols],
                        rhs=acodes[b][:, P * g : P * g + P].bitcast(FP8X4),
                        rhs_scale=ascales[b][:, P * g : P * g + P],
                        start=(g == 0),
                        stop=(g == 1),
                    )
            ax_ps[b, h] = acc

        def ax_copy(b, h):
            axt = rot.tile([P, 512], BF16, name="axt%d" % h, align_bytes=64)
            src = ax_ps[b, h][:].rearrange("p a r -> p r a")
            dst = axt[:].rearrange("p (r a) -> p r a", a=4)
            if b >= 2 and b % 2 == 1 and h == 0:
                nc.vector.tensor_copy(out=dst, in_=src)
            else:
                nc.scalar.copy(dst, src)
            axg[b, h] = axt

        def axq(b, h):
            if b not in axc:
                cod = rot.tile([P, 256], U32, align_bytes=64)
                sca = rot.tile([P, 256], U8, align_bytes=64)
                axc[b] = cod
                axs[b] = sca
            cols = slice(P * h, P * h + P)
            nc.vector.quantize_mx(out=axc[b][:, cols].bitcast(FP8X4), scales=axs[b][:, cols], in_=axg[b, h][:])

        o_ps, o_sb = {}, {}

        def s2(b, f):
            acc = ps_o.tile([P, 512], F32, tag="acc")
            for h in range(2):
                cols = slice(P * h, P * h + P)
                nc.tensor.matmul_mx(
                    out=acc[:],
                    lhsT=axc[b][:, cols].bitcast(FP8X4),
                    lhsT_scale=axs[b][:, cols],
                    rhs=w[:, h, 1024 * f : 1024 * f + 1024].bitcast(FP4X4),
                    rhs_scale=wsc[:, h, 512 * f : 512 * f + 512],
                    start=(h == 0),
                    stop=(h == 1),
                )
            o_ps[b, f] = acc

        def o_copy(b, f):
            if f == 0:
                ot = rot.tile([P, N], F32)
                o_sb[b] = ot
            if b == NB - 1 and f == 1:
                for z in range(2):
                    cols = slice(512 + 256 * z, 768 + 256 * z)
                    part = o_ps[b, f][:, 256 * z : 256 * z + 256]
                    if z == 0:
                        nc.vector.tensor_copy(out=o_sb[b][:, cols], in_=part)
                    else:
                        nc.scalar.copy(o_sb[b][:, cols], part)
                    nc.sync.dma_start(out=rows[b][:, cols], in_=o_sb[b][:, cols])
                return
            dst = o_sb[b][:, 512 * f : 512 * f + 512]
            if f == 1:
                nc.vector.tensor_copy(out=dst, in_=o_ps[b, f][:])
            else:
                nc.scalar.copy(dst, o_ps[b, f][:])
            nc.sync.dma_start(out=rows[b][:, 512 * f : 512 * f + 512], in_=dst)

        ones = keep.tile([P, 512], BF16, align_bytes=64)
        nc.vector.memset(ones[:], 1.0)

        def warm(n):
            for i in range(n):
                acc = ps_o.tile([P, 512], F32, tag="acc")
                nc.tensor.matmul(acc[:], lhsT=ones[:, 0:P], rhs=ones[:], start=True, stop=True)

        def s_xi(g, h, lo, hi):
            x_inter("S", g, h, lo, hi)

        def v_xi(g, h, lo, hi):
            x_inter("V", g, h, lo, hi)

        s_xi(0, 0, 0, 16)
        sc_transposes()
        v_xi(0, 0, 32, 64)
        s_xi(0, 0, 16, 32)
        sc_copy(0)
        sc_copy(1)
        x_quant(0, 0)
        prod(0)
        tp(0)
        warm(2)
        s_xi(1, 0, 16, 48)
        s_xi(0, 1, 32, 48)
        v_xi(0, 1, 48, 64)
        s_xi(1, 0, 0, 16)
        s_xi(0, 1, 0, 16)
        s_xi(1, 1, 16, 32)
        v_xi(1, 0, 48, 64)
        prod(1)
        tp(1)
        warm(2)
        prod(2)
        tcopy(0)
        prod(3)
        tcopy(1)
        aq(0)
        s_xi(1, 1, 48, 64)
        x_quant(1, 0)
        tp(2)
        warm(1)
        v_xi(0, 1, 16, 32)
        s_xi(1, 1, 0, 16)
        aq(1)
        tp(3)
        warm(1)
        s1(0, 0)
        s1(1, 0)
        x_quant(0, 1)
        tcopy(2)
        s_xi(1, 1, 32, 48)
        aq(2)
        s1(2, 0)
        x_quant(1, 1)
        ax_copy(0, 0)
        s1(0, 1)
        ax_copy(1, 0)
        s1(1, 1)
        prod(4)
        axq(0, 0)
        perm(4)
        tp(4)
        ax_copy(0, 1)
        s1(2, 1)
        ax_copy(1, 1)
        tcopy(3)
        axq(0, 1)

        def at(fn, b, *args):
            if 0 <= b < NB:
                fn(b, *args)

        for b in range(NB):
            at(o_copy, b - 1, 0)
            s2(b, 0)
            at(axq, b + 1, 0)
            at(axq, b + 1, 1)
            s2(b, 1)
            at(ax_copy, b + 2, 1)
            at(aq, b + 3)
            at(s1, b + 3, 1)
            at(s1, b + 3, 0)
            at(tcopy, b + 4)
            at(prod, b + 5)
            at(o_copy, b - 1, 1)
            at(perm, b + 5)
            at(tp, b + 5)
            at(ax_copy, b + 2, 0)
        o_copy(NB - 1, 0)
        o_copy(NB - 1, 1)
